import numpy as np
import ml_dtypes


def mxq(x, axis, fmt="e4m3"):
    dtype, down = {"e4m3": (ml_dtypes.float8_e4m3fn, 7), "e5m2": (ml_dtypes.float8_e5m2, 14)}[fmt]
    v = np.moveaxis(np.asarray(x, np.float32).astype(ml_dtypes.bfloat16).astype(np.float64), axis, -1)
    blocks = v.reshape(v.shape[:-1] + (-1, 32))
    amax = np.abs(blocks).max(-1, keepdims=True)
    byte = np.maximum(np.where(amax > 0, np.frexp(amax)[1] - 1 + 127, 0) - down, 1)
    scale = np.exp2(byte - 127.0)
    codes = (blocks / scale).astype(np.float32).astype(dtype).astype(np.float64)
    return np.moveaxis((codes * scale).reshape(v.shape), -1, axis)


WIDE = False


def mx_kscale(k):
    if not WIDE:
        return np.ones(k)
    levels = np.array([10, -10, 5, -5, 0])
    a = np.random.permutation(np.resize(levels, k // 512 * 4)).reshape(k // 512, 4)
    idx = np.arange(k)
    return np.exp2(a[idx // 512, idx % 128 // 32])


BF16 = ml_dtypes.bfloat16


def bf(x):
    return np.asarray(x, np.float32).astype(BF16)


def f64(x):
    return np.asarray(x).astype(np.float64)


E2M1 = np.array([0.0, 0.5, 1.0, 1.5, 2.0, 3.0, 4.0, 6.0, -0.0, -0.5, -1.0, -1.5, -2.0, -3.0, -4.0, -6.0])


def pack_weight(w, fmt):
    k, n = w.shape
    w = f64(bf(w)).reshape(k // 32, 32, n)
    amax = np.abs(w).max(1)
    if fmt == "e4m3":
        byte = np.frexp(amax)[1] - 1 + 127 - 7
    else:
        mant, ex = np.frexp(amax / 6.0)
        byte = np.where(mant > 0.5, ex, ex - 1) + 127
    byte = np.clip(np.where(amax > 0, byte, 1), 1, 254)
    scaled = (w * np.exp2(127.0 - byte)[:, None, :]).reshape(k, n).astype(np.float32)
    by_word = np.ascontiguousarray(scaled.reshape(k // 512, 128, 4, n).transpose(0, 1, 3, 2))
    if fmt == "e4m3":
        words = by_word.astype(ml_dtypes.float8_e4m3fn).view(np.uint8)
    else:
        c = by_word.astype(ml_dtypes.float4_e2m1fn).view(np.uint8) & 0xF
        words = c[..., 0::2] | (c[..., 1::2] << 4)
    return np.ascontiguousarray(words), np.ascontiguousarray(byte.astype(np.uint8).reshape(k // 512, 16, n))


def unpack_weight(words, scales, fmt):
    g, p, n, _ = words.shape
    if fmt == "e4m3":
        vals = np.ascontiguousarray(words).view(ml_dtypes.float8_e4m3fn).astype(np.float64)
    else:
        nib = np.empty((g, p, n, 4), np.uint8)
        nib[..., 0::2] = words & 0xF
        nib[..., 1::2] = words >> 4
        vals = E2M1[nib]
    vals = vals * np.repeat(np.exp2(scales.astype(np.float64) - 127.0), 8, axis=1)[..., None]
    return vals.transpose(0, 1, 3, 2).reshape(g * 512, n)


B, U, I, H = 4096, 4, 512, 128


def sigmoid(v):
    return 1.0 / (1.0 + np.exp(-v))


def setup_inputs():
    s = mx_kscale(I)
    inputs = bf(np.random.standard_normal((B, U, I)) * s)
    hidden = bf(np.random.standard_normal((B, U, H)))
    w_ih = np.random.standard_normal((U, 3 * H, I)) / np.sqrt(I) / s
    cat = np.ascontiguousarray(w_ih.swapaxes(1, 2)).reshape(-1, 3 * H)
    words, scales = pack_weight(cat, "e4m3")
    w_hh = bf(np.random.standard_normal((U, 3 * H, H)) / np.sqrt(H))
    b_ih = bf(np.random.standard_normal((U, 3 * H)) * 0.3)
    b_hh = bf(np.random.standard_normal((U, 3 * H)) * 0.3)
    return {"inputs": inputs,
            "hidden": hidden,
            "w_ih_words": words,
            "w_ih_scales": scales,
            "w_hh": w_hh,
            "b_ih": b_ih,
            "b_hh": b_hh}


def reference(inputs, hidden, w_ih_words, w_ih_scales, w_hh, b_ih, b_hh):
    h = f64(hidden)
    gx = (mxq(f64(inputs), 2, "e4m3").transpose(1, 0, 2) @ unpack_weight(w_ih_words, w_ih_scales, "e4m3").reshape(U, I, 3 * H)).transpose(1, 0, 2) + f64(b_ih)
    gh = (h.transpose(1, 0, 2) @ f64(w_hh).transpose(0, 2, 1)).transpose(1, 0, 2) + f64(b_hh)
    xr, xz, xn = gx[..., :H], gx[..., H:2 * H], gx[..., 2 * H:]
    hr, hz, hn = gh[..., :H], gh[..., H:2 * H], gh[..., 2 * H:]
    r = sigmoid(xr + hr)
    z = sigmoid(xz + hz)
    n = np.tanh(xn + r * hn)
    return (1.0 - z) * n + z * h

@@ -1,0 +1,283 @@
+from contextlib import ExitStack
+
+import concourse.mybir as mybir
+from concourse.masks import make_identity
+
+F32 = mybir.dt.float32
+BF16 = mybir.dt.bfloat16
+I32 = mybir.dt.int32
+U32 = mybir.dt.uint32
+U8 = mybir.dt.uint8
+FP8X4 = mybir.dt.float8_e4m3fn_x4
+ACT = mybir.ActivationFunctionType
+ALU = mybir.AluOpType
+
+BATCH, UNITS, K_IN, HID = 4096, 4, 512, 128
+P = 128
+GATES = 3
+RESET, UPDATE, NEW = 0, 1, 2
+ROW_GROUPS = 4
+CHUNK = P * ROW_GROUPS
+N_CHUNKS = (BATCH // CHUNK) * UNITS
+WORDS = K_IN // 2
+HALF = CHUNK // 2
+
+AHEAD_LOAD = 4
+AHEAD_IN = 2
+BEHIND_CAND = 1
+BEHIND_BLEND = 2
+BEHIND_OUT = 3
+
+FLOPS = 2 * BATCH * UNITS * (K_IN + HID) * GATES * HID
+
+
+def tile_grouptorchgru_t_e_kernel(
+    tc, inputs, hidden, w_ih_words, w_ih_scales, w_hh, b_ih, b_hh, out
+):
+    nc = tc.nc
+    with ExitStack() as ctx:
+        ctx.enter_context(tc.manual_schedule())
+        const = ctx.enter_context(tc.tile_pool(name="const", bufs=1))
+        x_pool = ctx.enter_context(tc.tile_pool(name="x", bufs=4))
+        hid_pool = ctx.enter_context(tc.tile_pool(name="hid", bufs=4))
+        mx_pool = ctx.enter_context(tc.tile_pool(name="mx", bufs=5))
+        ht_pool = ctx.enter_context(tc.tile_pool(name="ht", bufs=6))
+        work = ctx.enter_context(tc.tile_pool(name="work", bufs=2))
+        late = ctx.enter_context(tc.tile_pool(name="late", bufs=4))
+        psum = ctx.enter_context(tc.psum_pool(name="psum", bufs=8))
+
+        x_of, hid_of, grouped_of, codes_of, planes_of, ht_of = {}, {}, {}, {}, {}, {}
+        gh_of, gx_of, pre_of, rz_of, gated_of, cand_of, blend_of = {}, {}, {}, {}, {}, {}, {}
+
+        def batch_rows(c):
+            first = (c // UNITS) * CHUNK
+            return slice(first, first + CHUNK)
+
+        def load(c):
+            block, u = divmod(c, UNITS)
+            if u == 0:
+                hid = hid_pool.tile([P, ROW_GROUPS, UNITS, HID], BF16)
+                nc.sync.dma_start(
+                    out=hid[:],
+                    in_=hidden[batch_rows(c), :, :].rearrange("(p j) u h -> p j u h", j=ROW_GROUPS),
+                )
+                hid_of[block] = hid
+            x = x_pool.tile([P, ROW_GROUPS, K_IN], BF16)
+            nc.sync.dma_start(
+                out=x[:],
+                in_=inputs[batch_rows(c), u, :].rearrange("(p j) k -> p j k", j=ROW_GROUPS),
+            )
+            x_of[c] = x
+
+        def transpose_in(c):
+            block, u = divmod(c, UNITS)
+            x_words = x_of[c][:].bitcast(F32)
+            grouped = work.tile([P, CHUNK * 4], BF16, align_bytes=64)
+            grouped_words = grouped[:].bitcast(F32).rearrange("p (r w) -> p r w", w=2)
+            grouped_of[c] = grouped
+
+            def transpose_half(half, copy):
+                xt = psum.tile([P, 2, HALF], F32, tag="bank")
+                for jj in range(2):
+                    for w in range(2):
+                        nc.tensor.transpose(
+                            xt[:, w, jj * P : (jj + 1) * P],
+                            x_words[:, 2 * half + jj, w:WORDS:2],
+                            ident_f32[:],
+                        )
+                copy(
+                    out=grouped_words[:, half * HALF : (half + 1) * HALF, :],
+                    in_=xt[:].rearrange("p w r -> p r w"),
+                )
+
+            transpose_half(0, nc.scalar.copy)
+            ht_ps = psum.tile([P, CHUNK], BF16, tag="bank")
+            for j in range(ROW_GROUPS):
+                nc.tensor.transpose(
+                    ht_ps[:, j * P : (j + 1) * P], hid_of[block][:, j, u, :], ident_bf[:]
+                )
+            ht = ht_pool.tile([P, CHUNK], BF16)
+            nc.scalar.copy(out=ht[:], in_=ht_ps[:])
+            ht_of[c] = ht
+            transpose_half(1, nc.vector.tensor_copy)
+
+        def quantise(c):
+            codes = mx_pool.tile([P, CHUNK], U32, align_bytes=64)
+            planes = mx_pool.tile([P, CHUNK], U8, align_bytes=64)
+            nc.vector.quantize_mx(
+                out=codes[:].bitcast(FP8X4), scales=planes[:], in_=grouped_of[c][:]
+            )
+            codes_of[c] = codes
+            planes_of[c] = planes
+
+        def matmul_hidden(c, gate):
+            u = c % UNITS
+            gh = psum.tile([P, CHUNK], F32, tag="bank")
+            nc.tensor.matmul(
+                out=gh[:], lhsT=whh_t[:, u * GATES + gate, :], rhs=ht_of[c][:], start=True, stop=True
+            )
+            gh_of[c, gate] = gh
+
+        def matmul_inputs(c, gate):
+            u = c % UNITS
+            cols = slice(gate * HID, (gate + 1) * HID)
+            gx = psum.tile([P, CHUNK], F32, tag="bank")
+            nc.tensor.matmul_mx(
+                out=gx[:],
+                lhsT=w_words[:, u, cols].bitcast(FP8X4),
+                lhsT_scale=w_planes[:, u, cols],
+                rhs=codes_of[c][:].bitcast(FP8X4),
+                rhs_scale=planes_of[c][:],
+                start=True,
+                stop=True,
+            )
+            gx_of[c, gate] = gx
+
+        def sum_reset_update(c):
+            u = c % UNITS
+            pre = work.tile([P, 2, CHUNK], F32)
+            r_col = u * GATES + RESET
+            z_col = u * GATES + UPDATE
+            nc.scalar.activation(
+                out=pre[:, RESET, :], in_=gh_of[c, RESET][:], func=ACT.Identity,
+                bias=bias_sum[:, r_col : r_col + 1], scale=1.0,
+            )
+            nc.scalar.activation(
+                out=pre[:, UPDATE, :], in_=gh_of[c, UPDATE][:], func=ACT.Identity,
+                bias=bias_neg[:, z_col : z_col + 1], scale=-1.0,
+            )
+            nc.vector.tensor_tensor(
+                out=pre[:, RESET, :], in0=pre[:, RESET, :], in1=gx_of[c, RESET][:], op=ALU.add
+            )
+            nc.vector.tensor_tensor(
+                out=pre[:, UPDATE, :], in0=pre[:, UPDATE, :], in1=gx_of[c, UPDATE][:], op=ALU.subtract
+            )
+            pre_of[c] = pre
+
+        def sigmoids(c):
+            rz = late.tile([P, 2, CHUNK], F32)
+            nc.scalar.activation(out=rz[:], in_=pre_of[c][:], func=ACT.Sigmoid)
+            rz_of[c] = rz
+
+        def gate_hidden(c):
+            n_col = (c % UNITS) * GATES + NEW
+            gated = work.tile([P, CHUNK], F32)
+            nc.vector.scalar_tensor_tensor(
+                out=gated[:], in0=gh_of[c, NEW][:], scalar=bias_hh[:, n_col : n_col + 1],
+                in1=rz_of[c][:, RESET, :], op0=ALU.add, op1=ALU.mult,
+            )
+            gated_of[c] = gated
+
+        def sum_candidate(c):
+            cand = work.tile([P, CHUNK], F32)
+            nc.vector.tensor_tensor(
+                out=cand[:], in0=gated_of[c][:], in1=gx_of[c, NEW][:], op=ALU.add
+            )
+            cand_of[c] = cand
+
+        def blend(c):
+            n_col = (c % UNITS) * GATES + NEW
+            new = work.tile([P, CHUNK], F32)
+            nc.scalar.activation(
+                out=new[:], in_=cand_of[c][:], func=ACT.Tanh,
+                bias=bias_ih[:, n_col : n_col + 1], scale=1.0,
+            )
+            diff = work.tile([P, CHUNK], F32)
+            nc.gpsimd.tensor_tensor(out=diff[:], in0=new[:], in1=ht_of[c][:], op=ALU.subtract)
+            mixed = late.tile([P, CHUNK], F32)
+            nc.gpsimd.tensor_tensor(out=mixed[:], in0=rz_of[c][:, UPDATE, :], in1=diff[:], op=ALU.mult)
+            blend_of[c] = mixed
+
+        def transpose_out(c):
+            block, u = divmod(c, UNITS)
+            back = psum.tile([P, ROW_GROUPS, HID], F32, tag="bank")
+            for j in range(ROW_GROUPS):
+                nc.tensor.transpose(
+                    back[:, j, :], blend_of[c][:, j * P : (j + 1) * P], ident_f32[:]
+                )
+            result = late.tile([P, ROW_GROUPS, HID], F32)
+            nc.vector.tensor_tensor(
+                out=result[:], in0=back[:], in1=hid_of[block][:, :, u, :], op=ALU.add
+            )
+            nc.sync.dma_start(
+                out=out[batch_rows(c), u, :].rearrange("(p j) h -> p j h", j=ROW_GROUPS),
+                in_=result[:],
+            )
+
+        def run(stage, c, *args):
+            if 0 <= c < N_CHUNKS:
+                stage(c, *args)
+
+        warm = const.tile([P, 1], F32)
+        nc.vector.memset(warm[:], 0.0)
+        nc.scalar.activation(out=warm[:], in_=warm[:], func=ACT.Sigmoid)
+
+        ident_f32 = const.tile([P, P], F32)
+        make_identity(nc, ident_f32[:])
+        ident_bf = const.tile([P, P], BF16)
+        make_identity(nc, ident_bf[:])
+
+        w_planes = const.tile([P, UNITS, GATES * HID], U8, align_bytes=64)
+        nc.vector.memset(w_planes[:].bitcast(I32), 0)
+        bias_rows = const.tile([P, P], BF16)
+        nc.vector.memset(bias_rows[:], 0.0)
+
+        load(0)
+        for quadrant in range(4):
+            nc.sync.dma_start(
+                out=w_planes[32 * quadrant : 32 * quadrant + 4, :, :].bitcast(I32),
+                in_=w_ih_scales[:, 4 * quadrant : 4 * quadrant + 4, :]
+                .rearrange("u q n -> q u n")
+                .bitcast(I32),
+            )
+        w_words = const.tile([P, UNITS, GATES * HID], U32, align_bytes=64)
+        nc.sync.dma_start(
+            out=w_words[:].bitcast(I32),
+            in_=w_ih_words.rearrange("u p n t -> p u (n t)").bitcast(I32),
+        )
+        whh_rows = const.tile([P, UNITS * GATES, HID], BF16)
+        nc.sync.dma_start(out=whh_rows[:], in_=w_hh.rearrange("u (g m) k -> m (u g) k", m=P))
+        n_bias = UNITS * GATES
+        nc.sync.dma_start(out=bias_rows[0:n_bias, :], in_=b_ih.rearrange("u (g h) -> (u g) h", h=HID))
+        nc.sync.dma_start(
+            out=bias_rows[n_bias : 2 * n_bias, :], in_=b_hh.rearrange("u (g h) -> (u g) h", h=HID)
+        )
+        for c in range(1, AHEAD_LOAD - AHEAD_IN + 1):
+            load(c)
+
+        transpose_in(0)
+        quantise(0)
+
+        whh_t = const.tile([P, UNITS * GATES, P], BF16)
+        for u in range(UNITS):
+            whh_ps = psum.tile([P, GATES, P], BF16, tag="bank")
+            for gate in range(GATES):
+                nc.tensor.transpose(whh_ps[:, gate, :], whh_rows[:, u * GATES + gate, :], ident_bf[:])
+            nc.vector.tensor_copy(out=whh_t[:, u * GATES : (u + 1) * GATES, :], in_=whh_ps[:])
+        bias_ps = psum.tile([P, P], BF16, tag="bank")
+        nc.tensor.transpose(bias_ps[:], bias_rows[:], ident_bf[:])
+        bias_ih = const.tile([P, n_bias], F32)
+        nc.vector.tensor_copy(out=bias_ih[:], in_=bias_ps[:, 0:n_bias])
+        bias_hh = const.tile([P, n_bias], F32)
+        nc.vector.tensor_copy(out=bias_hh[:], in_=bias_ps[:, n_bias : 2 * n_bias])
+        bias_sum = const.tile([P, n_bias], F32)
+        nc.vector.tensor_tensor(out=bias_sum[:], in0=bias_ih[:], in1=bias_hh[:], op=ALU.add)
+        bias_neg = const.tile([P, n_bias], F32)
+        nc.vector.tensor_scalar_mul(out=bias_neg[:], in0=bias_sum[:], scalar1=-1.0)
+
+        for i in range(1 - AHEAD_IN, N_CHUNKS + BEHIND_OUT):
+            run(load, i + AHEAD_LOAD)
+            run(matmul_hidden, i, RESET)
+            run(matmul_hidden, i, UPDATE)
+            run(matmul_hidden, i - BEHIND_CAND, NEW)
+            run(matmul_inputs, i, RESET)
+            run(matmul_inputs, i, UPDATE)
+            run(matmul_inputs, i - BEHIND_CAND, NEW)
+            run(sum_reset_update, i)
+            run(blend, i - BEHIND_BLEND)
+            run(gate_hidden, i - BEHIND_CAND)
+            run(transpose_in, i + AHEAD_IN)
+            run(sum_candidate, i - BEHIND_CAND)
+            run(sigmoids, i)
+            run(transpose_out, i - BEHIND_OUT)
+            run(quantise, i + AHEAD_IN)

@@ -69,28 +69,27 @@ def tile_grouptorchgru_t_e_kernel(
             )
             x_of[c] = x
 
-        def transpose_in(c):
-            block, u = divmod(c, UNITS)
+        def transpose_inputs(c, half, copy):
+            if half == 0:
+                grouped = work.tile([P, CHUNK * 4], BF16, align_bytes=64)
+                grouped_of[c] = grouped
             x_words = x_of[c][:].bitcast(F32)
-            grouped = work.tile([P, CHUNK * 4], BF16, align_bytes=64)
-            grouped_words = grouped[:].bitcast(F32).rearrange("p (r w) -> p r w", w=2)
-            grouped_of[c] = grouped
+            grouped_words = grouped_of[c][:].bitcast(F32).rearrange("p (r w) -> p r w", w=2)
+            xt = psum.tile([P, 2, HALF], F32, tag="bank")
+            for jj in range(2):
+                for w in range(2):
+                    nc.tensor.transpose(
+                        xt[:, w, jj * P : (jj + 1) * P],
+                        x_words[:, 2 * half + jj, w:WORDS:2],
+                        ident_f32[:],
+                    )
+            copy(
+                out=grouped_words[:, half * HALF : (half + 1) * HALF, :],
+                in_=xt[:].rearrange("p w r -> p r w"),
+            )
 
-            def transpose_half(half, copy):
-                xt = psum.tile([P, 2, HALF], F32, tag="bank")
-                for jj in range(2):
-                    for w in range(2):
-                        nc.tensor.transpose(
-                            xt[:, w, jj * P : (jj + 1) * P],
-                            x_words[:, 2 * half + jj, w:WORDS:2],
-                            ident_f32[:],
-                        )
-                copy(
-                    out=grouped_words[:, half * HALF : (half + 1) * HALF, :],
-                    in_=xt[:].rearrange("p w r -> p r w"),
-                )
-
-            transpose_half(0, nc.scalar.copy)
+        def transpose_hidden(c):
+            block, u = divmod(c, UNITS)
             ht_ps = psum.tile([P, CHUNK], BF16, tag="bank")
             for j in range(ROW_GROUPS):
                 nc.tensor.transpose(
@@ -99,7 +98,6 @@ def tile_grouptorchgru_t_e_kernel(
             ht = ht_pool.tile([P, CHUNK], BF16)
             nc.scalar.copy(out=ht[:], in_=ht_ps[:])
             ht_of[c] = ht
-            transpose_half(1, nc.vector.tensor_copy)
 
         def quantise(c):
             codes = mx_pool.tile([P, CHUNK], U32, align_bytes=64)
@@ -245,7 +243,9 @@ def tile_grouptorchgru_t_e_kernel(
         for c in range(1, AHEAD_LOAD - AHEAD_IN + 1):
             load(c)
 
-        transpose_in(0)
+        transpose_inputs(0, 0, nc.scalar.copy)
+        transpose_hidden(0)
+        transpose_inputs(0, 1, nc.vector.tensor_copy)
         quantise(0)
 
         whh_t = const.tile([P, UNITS * GATES, P], BF16)
@@ -268,15 +268,17 @@ def tile_grouptorchgru_t_e_kernel(
         for i in range(1 - AHEAD_IN, N_CHUNKS + BEHIND_OUT):
             run(load, i + AHEAD_LOAD)
             run(matmul_hidden, i, RESET)
-            run(matmul_hidden, i, UPDATE)
-            run(matmul_hidden, i - BEHIND_CAND, NEW)
             run(matmul_inputs, i, RESET)
             run(matmul_inputs, i, UPDATE)
-            run(matmul_inputs, i - BEHIND_CAND, NEW)
+            run(matmul_hidden, i, UPDATE)
             run(sum_reset_update, i)
             run(blend, i - BEHIND_BLEND)
+            run(transpose_inputs, i + AHEAD_IN, 0, nc.scalar.copy)
+            run(transpose_hidden, i + AHEAD_IN)
+            run(matmul_hidden, i - BEHIND_CAND, NEW)
+            run(matmul_inputs, i - BEHIND_CAND, NEW)
             run(gate_hidden, i - BEHIND_CAND)
-            run(transpose_in, i + AHEAD_IN)
+            run(transpose_inputs, i + AHEAD_IN, 1, nc.vector.tensor_copy)
             run(sum_candidate, i - BEHIND_CAND)
             run(sigmoids, i)
             run(transpose_out, i - BEHIND_OUT)

@@ -88,7 +88,7 @@ def tile_grouptorchgru_t_e_kernel(
                 in_=xt[:].rearrange("p w r -> p r w"),
             )
 
-        def transpose_hidden(c):
+        def transpose_hidden(c, copy):
             block, u = divmod(c, UNITS)
             ht_ps = psum.tile([P, CHUNK], BF16, tag="bank")
             for j in range(ROW_GROUPS):
@@ -96,7 +96,7 @@ def tile_grouptorchgru_t_e_kernel(
                     ht_ps[:, j * P : (j + 1) * P], hid_of[block][:, j, u, :], ident_bf[:]
                 )
             ht = ht_pool.tile([P, CHUNK], BF16)
-            nc.scalar.copy(out=ht[:], in_=ht_ps[:])
+            copy(out=ht[:], in_=ht_ps[:])
             ht_of[c] = ht
 
         def quantise(c):
@@ -244,7 +244,7 @@ def tile_grouptorchgru_t_e_kernel(
             load(c)
 
         transpose_inputs(0, 0, nc.scalar.copy)
-        transpose_hidden(0)
+        transpose_hidden(0, nc.scalar.copy)
         transpose_inputs(0, 1, nc.vector.tensor_copy)
         quantise(0)
 
@@ -274,11 +274,17 @@ def tile_grouptorchgru_t_e_kernel(
             run(sum_reset_update, i)
             run(blend, i - BEHIND_BLEND)
             run(transpose_inputs, i + AHEAD_IN, 0, nc.scalar.copy)
-            run(transpose_hidden, i + AHEAD_IN)
+            if (i + AHEAD_IN) % 2 == 0:
+                run(transpose_hidden, i + AHEAD_IN, nc.scalar.copy)
+            else:
+                run(transpose_inputs, i + AHEAD_IN, 1, nc.scalar.copy)
             run(matmul_hidden, i - BEHIND_CAND, NEW)
             run(matmul_inputs, i - BEHIND_CAND, NEW)
             run(gate_hidden, i - BEHIND_CAND)
-            run(transpose_inputs, i + AHEAD_IN, 1, nc.vector.tensor_copy)
+            if (i + AHEAD_IN) % 2 == 0:
+                run(transpose_inputs, i + AHEAD_IN, 1, nc.vector.tensor_copy)
+            else:
+                run(transpose_hidden, i + AHEAD_IN, nc.vector.tensor_copy)
             run(sum_candidate, i - BEHIND_CAND)
             run(sigmoids, i)
             run(transpose_out, i - BEHIND_OUT)

@@ -55,6 +55,12 @@ def tile_grouptorchgru_t_e_kernel(
 
         def load(c):
             block, u = divmod(c, UNITS)
+            x = x_pool.tile([P, ROW_GROUPS, K_IN], BF16)
+            nc.sync.dma_start(
+                out=x[:],
+                in_=inputs[batch_rows(c), u, :].rearrange("(p j) k -> p j k", j=ROW_GROUPS),
+            )
+            x_of[c] = x
             if u == 0:
                 hid = hid_pool.tile([P, ROW_GROUPS, UNITS, HID], BF16)
                 nc.sync.dma_start(
@@ -62,12 +68,6 @@ def tile_grouptorchgru_t_e_kernel(
                     in_=hidden[batch_rows(c), :, :].rearrange("(p j) u h -> p j u h", j=ROW_GROUPS),
                 )
                 hid_of[block] = hid
-            x = x_pool.tile([P, ROW_GROUPS, K_IN], BF16)
-            nc.sync.dma_start(
-                out=x[:],
-                in_=inputs[batch_rows(c), u, :].rearrange("(p j) k -> p j k", j=ROW_GROUPS),
-            )
-            x_of[c] = x
 
         def transpose_inputs(c, half, copy):
             if half == 0:
@@ -180,10 +180,11 @@ def tile_grouptorchgru_t_e_kernel(
                 out=new[:], in_=cand_of[c][:], func=ACT.Tanh,
                 bias=bias_ih[:, n_col : n_col + 1], scale=1.0,
             )
+            engine = nc.vector if c == N_CHUNKS - 1 else nc.gpsimd
             diff = work.tile([P, CHUNK], F32)
-            nc.gpsimd.tensor_tensor(out=diff[:], in0=new[:], in1=ht_of[c][:], op=ALU.subtract)
+            engine.tensor_tensor(out=diff[:], in0=new[:], in1=ht_of[c][:], op=ALU.subtract)
             mixed = late.tile([P, CHUNK], F32)
-            nc.gpsimd.tensor_tensor(out=mixed[:], in0=rz_of[c][:, UPDATE, :], in1=diff[:], op=ALU.mult)
+            engine.tensor_tensor(out=mixed[:], in0=rz_of[c][:, UPDATE, :], in1=diff[:], op=ALU.mult)
             blend_of[c] = mixed
 
         def transpose_out(c):
@@ -221,6 +222,13 @@ def tile_grouptorchgru_t_e_kernel(
         nc.vector.memset(bias_rows[:], 0.0)
 
         load(0)
+        whh_rows = const.tile([P, UNITS * GATES, HID], BF16)
+        nc.sync.dma_start(out=whh_rows[:], in_=w_hh.rearrange("u (g m) k -> m (u g) k", m=P))
+        n_bias = UNITS * GATES
+        nc.sync.dma_start(out=bias_rows[0:n_bias, :], in_=b_ih.rearrange("u (g h) -> (u g) h", h=HID))
+        nc.sync.dma_start(
+            out=bias_rows[n_bias : 2 * n_bias, :], in_=b_hh.rearrange("u (g h) -> (u g) h", h=HID)
+        )
         for quadrant in range(4):
             nc.sync.dma_start(
                 out=w_planes[32 * quadrant : 32 * quadrant + 4, :, :].bitcast(I32),
@@ -229,19 +237,19 @@ def tile_grouptorchgru_t_e_kernel(
                 .bitcast(I32),
             )
         w_words = const.tile([P, UNITS, GATES * HID], U32, align_bytes=64)
-        nc.sync.dma_start(
-            out=w_words[:].bitcast(I32),
-            in_=w_ih_words.rearrange("u p n t -> p u (n t)").bitcast(I32),
-        )
-        whh_rows = const.tile([P, UNITS * GATES, HID], BF16)
-        nc.sync.dma_start(out=whh_rows[:], in_=w_hh.rearrange("u (g m) k -> m (u g) k", m=P))
-        n_bias = UNITS * GATES
-        nc.sync.dma_start(out=bias_rows[0:n_bias, :], in_=b_ih.rearrange("u (g h) -> (u g) h", h=HID))
-        nc.sync.dma_start(
-            out=bias_rows[n_bias : 2 * n_bias, :], in_=b_hh.rearrange("u (g h) -> (u g) h", h=HID)
-        )
-        for c in range(1, AHEAD_LOAD - AHEAD_IN + 1):
-            load(c)
+
+        def load_words(u):
+            nc.sync.dma_start(
+                out=w_words[:, u, :].bitcast(I32),
+                in_=w_ih_words[u].rearrange("p n t -> p (n t)").bitcast(I32),
+            )
+
+        load_words(0)
+        load(1)
+        load(2)
+        for u in range(1, UNITS):
+            load_words(u)
+        load(3)
 
         transpose_inputs(0, 0, nc.scalar.copy)
         transpose_hidden(0, nc.scalar.copy)
@@ -249,29 +257,38 @@ def tile_grouptorchgru_t_e_kernel(
         quantise(0)
 
         whh_t = const.tile([P, UNITS * GATES, P], BF16)
-        for u in range(UNITS):
-            whh_ps = psum.tile([P, GATES, P], BF16, tag="bank")
-            for gate in range(GATES):
-                nc.tensor.transpose(whh_ps[:, gate, :], whh_rows[:, u * GATES + gate, :], ident_bf[:])
-            nc.vector.tensor_copy(out=whh_t[:, u * GATES : (u + 1) * GATES, :], in_=whh_ps[:])
-        bias_ps = psum.tile([P, P], BF16, tag="bank")
-        nc.tensor.transpose(bias_ps[:], bias_rows[:], ident_bf[:])
         bias_ih = const.tile([P, n_bias], F32)
-        nc.vector.tensor_copy(out=bias_ih[:], in_=bias_ps[:, 0:n_bias])
         bias_hh = const.tile([P, n_bias], F32)
-        nc.vector.tensor_copy(out=bias_hh[:], in_=bias_ps[:, n_bias : 2 * n_bias])
         bias_sum = const.tile([P, n_bias], F32)
-        nc.vector.tensor_tensor(out=bias_sum[:], in0=bias_ih[:], in1=bias_hh[:], op=ALU.add)
         bias_neg = const.tile([P, n_bias], F32)
-        nc.vector.tensor_scalar_mul(out=bias_neg[:], in0=bias_sum[:], scalar1=-1.0)
 
-        for i in range(1 - AHEAD_IN, N_CHUNKS + BEHIND_OUT):
+        def prepare_weights():
+            for u in range(UNITS):
+                whh_ps = psum.tile([P, GATES, P], BF16, tag="bank")
+                for gate in range(GATES):
+                    nc.tensor.transpose(
+                        whh_ps[:, gate, :], whh_rows[:, u * GATES + gate, :], ident_bf[:]
+                    )
+                nc.vector.tensor_copy(out=whh_t[:, u * GATES : (u + 1) * GATES, :], in_=whh_ps[:])
+            bias_ps = psum.tile([P, P], BF16, tag="bank")
+            nc.tensor.transpose(bias_ps[:], bias_rows[:], ident_bf[:])
+            nc.vector.tensor_copy(out=bias_ih[:], in_=bias_ps[:, 0:n_bias])
+            nc.vector.tensor_copy(out=bias_hh[:], in_=bias_ps[:, n_bias : 2 * n_bias])
+            nc.vector.tensor_tensor(out=bias_sum[:], in0=bias_ih[:], in1=bias_hh[:], op=ALU.add)
+            nc.vector.tensor_scalar_mul(out=bias_neg[:], in0=bias_sum[:], scalar1=-1.0)
+
+        prepare_weights()
+        for i in range(N_CHUNKS + BEHIND_OUT):
             run(load, i + AHEAD_LOAD)
             run(matmul_hidden, i, RESET)
             run(matmul_inputs, i, RESET)
             run(matmul_inputs, i, UPDATE)
             run(matmul_hidden, i, UPDATE)
             run(sum_reset_update, i)
+            if i == 0:
+                transpose_inputs(1, 0, nc.scalar.copy)
+                transpose_inputs(1, 1, nc.vector.tensor_copy)
+                transpose_hidden(1, nc.scalar.copy)
             run(blend, i - BEHIND_BLEND)
             run(transpose_inputs, i + AHEAD_IN, 0, nc.scalar.copy)
             if (i + AHEAD_IN) % 2 == 0:
@@ -285,6 +302,8 @@ def tile_grouptorchgru_t_e_kernel(
                 run(transpose_inputs, i + AHEAD_IN, 1, nc.vector.tensor_copy)
             else:
                 run(transpose_hidden, i + AHEAD_IN, nc.vector.tensor_copy)
+            if i == 0:
+                quantise(1)
             run(sum_candidate, i - BEHIND_CAND)
             run(sigmoids, i)
             run(transpose_out, i - BEHIND_OUT)

@@ -44,10 +44,12 @@ def tile_grouptorchgru_t_e_kernel(
         ht_pool = ctx.enter_context(tc.tile_pool(name="ht", bufs=6))
         work = ctx.enter_context(tc.tile_pool(name="work", bufs=2))
         late = ctx.enter_context(tc.tile_pool(name="late", bufs=4))
+        mid = ctx.enter_context(tc.tile_pool(name="mid", bufs=3))
         psum = ctx.enter_context(tc.psum_pool(name="psum", bufs=8))
 
         x_of, hid_of, grouped_of, codes_of, planes_of, ht_of = {}, {}, {}, {}, {}, {}
-        gh_of, gx_of, pre_of, rz_of, gated_of, cand_of, blend_of = {}, {}, {}, {}, {}, {}, {}
+        gh_of, gx_of, pre_of, gated_of, cand_of, blend_of = {}, {}, {}, {}, {}, {}
+        xz_ps_of, xz_of, z_ps_of, reset_of, keep_of, new_of, diff_of = {}, {}, {}, {}, {}, {}, {}
 
         def batch_rows(c):
             first = (c // UNITS) * CHUNK
@@ -131,38 +133,76 @@ def tile_grouptorchgru_t_e_kernel(
             )
             gx_of[c, gate] = gx
 
-        def sum_reset_update(c):
+        def matmul_inputs_update(c):
             u = c % UNITS
-            pre = work.tile([P, 2, CHUNK], F32)
-            r_col = u * GATES + RESET
-            z_col = u * GATES + UPDATE
-            nc.scalar.activation(
-                out=pre[:, RESET, :], in_=gh_of[c, RESET][:], func=ACT.Identity,
-                bias=bias_sum[:, r_col : r_col + 1], scale=1.0,
+            cols = slice(UPDATE * HID, (UPDATE + 1) * HID)
+            xz_ps = psum.tile([P, ROW_GROUPS, HID], F32, tag="bank")
+            for j in range(ROW_GROUPS):
+                rows = slice(j * P, (j + 1) * P)
+                nc.tensor.matmul_mx(
+                    out=xz_ps[:, j, :],
+                    lhsT=codes_of[c][:, rows].bitcast(FP8X4),
+                    lhsT_scale=planes_of[c][:, rows],
+                    rhs=w_words[:, u, cols].bitcast(FP8X4),
+                    rhs_scale=w_planes[:, u, cols],
+                    start=True,
+                    stop=True,
+                )
+            xz_ps_of[c] = xz_ps
+
+        def copy_inputs_update(c):
+            xz = mid.tile([P, ROW_GROUPS, HID], F32)
+            nc.scalar.copy(out=xz[:], in_=xz_ps_of[c][:])
+            xz_of[c] = xz
+
+        def sum_update(c):
+            u = c % UNITS
+            z_ps = psum.tile([P, CHUNK], F32, tag="bank")
+            nc.tensor.matmul(
+                out=z_ps[:], lhsT=whh_t[:, u * GATES + UPDATE, :], rhs=ht_of[c][:],
+                start=True, stop=False,
             )
+            for j in range(ROW_GROUPS):
+                nc.tensor.matmul(
+                    out=z_ps[:, j * P : (j + 1) * P], lhsT=xz_of[c][:, j, :], rhs=ident_f32[:],
+                    is_transpose=True, start=False, stop=(j == ROW_GROUPS - 1),
+                )
+            z_ps_of[c] = z_ps
+
+        def sigmoid_update(c):
+            z_col = (c % UNITS) * GATES + UPDATE
+            keep = late.tile([P, CHUNK], F32)
             nc.scalar.activation(
-                out=pre[:, UPDATE, :], in_=gh_of[c, UPDATE][:], func=ACT.Identity,
+                out=keep[:], in_=z_ps_of[c][:], func=ACT.Sigmoid,
                 bias=bias_neg[:, z_col : z_col + 1], scale=-1.0,
             )
-            nc.vector.tensor_tensor(
-                out=pre[:, RESET, :], in0=pre[:, RESET, :], in1=gx_of[c, RESET][:], op=ALU.add
-            )
-            nc.vector.tensor_tensor(
-                out=pre[:, UPDATE, :], in0=pre[:, UPDATE, :], in1=gx_of[c, UPDATE][:], op=ALU.subtract
+            keep_of[c] = keep
+
+        def copy_hidden_reset(c):
+            r_col = (c % UNITS) * GATES + RESET
+            pre = work.tile([P, CHUNK], F32)
+            nc.scalar.activation(
+                out=pre[:], in_=gh_of[c, RESET][:], func=ACT.Identity,
+                bias=bias_sum[:, r_col : r_col + 1], scale=1.0,
             )
             pre_of[c] = pre
 
-        def sigmoids(c):
-            rz = late.tile([P, 2, CHUNK], F32)
-            nc.scalar.activation(out=rz[:], in_=pre_of[c][:], func=ACT.Sigmoid)
-            rz_of[c] = rz
+        def sum_reset(c):
+            nc.vector.tensor_tensor(
+                out=pre_of[c][:], in0=pre_of[c][:], in1=gx_of[c, RESET][:], op=ALU.add
+            )
+
+        def sigmoid_reset(c):
+            reset = mid.tile([P, CHUNK], F32)
+            nc.scalar.activation(out=reset[:], in_=pre_of[c][:], func=ACT.Sigmoid)
+            reset_of[c] = reset
 
         def gate_hidden(c):
             n_col = (c % UNITS) * GATES + NEW
             gated = work.tile([P, CHUNK], F32)
             nc.vector.scalar_tensor_tensor(
                 out=gated[:], in0=gh_of[c, NEW][:], scalar=bias_hh[:, n_col : n_col + 1],
-                in1=rz_of[c][:, RESET, :], op0=ALU.add, op1=ALU.mult,
+                in1=reset_of[c][:], op0=ALU.add, op1=ALU.mult,
             )
             gated_of[c] = gated
 
@@ -173,18 +213,23 @@ def tile_grouptorchgru_t_e_kernel(
             )
             cand_of[c] = cand
 
-        def blend(c):
+        def blend_engine(c):
+            return nc.vector if c == N_CHUNKS - 1 else nc.gpsimd
+
+        def candidate(c):
             n_col = (c % UNITS) * GATES + NEW
             new = work.tile([P, CHUNK], F32)
             nc.scalar.activation(
                 out=new[:], in_=cand_of[c][:], func=ACT.Tanh,
                 bias=bias_ih[:, n_col : n_col + 1], scale=1.0,
             )
-            engine = nc.vector if c == N_CHUNKS - 1 else nc.gpsimd
             diff = work.tile([P, CHUNK], F32)
-            engine.tensor_tensor(out=diff[:], in0=new[:], in1=ht_of[c][:], op=ALU.subtract)
+            blend_engine(c).tensor_tensor(out=diff[:], in0=new[:], in1=ht_of[c][:], op=ALU.subtract)
+            diff_of[c] = diff
+
+        def blend(c):
             mixed = late.tile([P, CHUNK], F32)
-            engine.tensor_tensor(out=mixed[:], in0=rz_of[c][:, UPDATE, :], in1=diff[:], op=ALU.mult)
+            blend_engine(c).tensor_tensor(out=mixed[:], in0=keep_of[c][:], in1=diff_of[c][:], op=ALU.mult)
             blend_of[c] = mixed
 
         def transpose_out(c):
@@ -282,29 +327,27 @@ def tile_grouptorchgru_t_e_kernel(
             run(load, i + AHEAD_LOAD)
             run(matmul_hidden, i, RESET)
             run(matmul_inputs, i, RESET)
-            run(matmul_inputs, i, UPDATE)
-            run(matmul_hidden, i, UPDATE)
-            run(sum_reset_update, i)
+            run(matmul_inputs_update, i)
+            run(matmul_inputs, i - BEHIND_CAND, NEW)
+            run(matmul_hidden, i - BEHIND_CAND, NEW)
+            run(copy_hidden_reset, i)
+            run(candidate, i - BEHIND_BLEND)
+            run(sum_reset, i)
+            run(copy_inputs_update, i)
+            run(gate_hidden, i - BEHIND_CAND)
             if i == 0:
                 transpose_inputs(1, 0, nc.scalar.copy)
                 transpose_inputs(1, 1, nc.vector.tensor_copy)
                 transpose_hidden(1, nc.scalar.copy)
-            run(blend, i - BEHIND_BLEND)
             run(transpose_inputs, i + AHEAD_IN, 0, nc.scalar.copy)
-            if (i + AHEAD_IN) % 2 == 0:
-                run(transpose_hidden, i + AHEAD_IN, nc.scalar.copy)
-            else:
-                run(transpose_inputs, i + AHEAD_IN, 1, nc.scalar.copy)
-            run(matmul_hidden, i - BEHIND_CAND, NEW)
-            run(matmul_inputs, i - BEHIND_CAND, NEW)
-            run(gate_hidden, i - BEHIND_CAND)
-            if (i + AHEAD_IN) % 2 == 0:
-                run(transpose_inputs, i + AHEAD_IN, 1, nc.vector.tensor_copy)
-            else:
-                run(transpose_hidden, i + AHEAD_IN, nc.vector.tensor_copy)
+            run(transpose_hidden, i + AHEAD_IN, nc.vector.tensor_copy)
+            run(sum_candidate, i - BEHIND_CAND)
+            run(sigmoid_reset, i)
+            run(sum_update, i - BEHIND_CAND)
+            run(sigmoid_update, i - BEHIND_CAND)
+            run(transpose_inputs, i + AHEAD_IN, 1, nc.vector.tensor_copy)
             if i == 0:
                 quantise(1)
-            run(sum_candidate, i - BEHIND_CAND)
-            run(sigmoids, i)
             run(transpose_out, i - BEHIND_OUT)
             run(quantise, i + AHEAD_IN)
+            run(blend, i - BEHIND_BLEND)

@@ -213,8 +213,11 @@ def tile_grouptorchgru_t_e_kernel(
             )
             cand_of[c] = cand
 
+        def on_gpsimd(c):
+            return c < N_CHUNKS - 2
+
         def blend_engine(c):
-            return nc.vector if c == N_CHUNKS - 1 else nc.gpsimd
+            return nc.gpsimd if on_gpsimd(c) else nc.vector
 
         def candidate(c):
             n_col = (c % UNITS) * GATES + NEW
@@ -223,8 +226,13 @@ def tile_grouptorchgru_t_e_kernel(
                 out=new[:], in_=cand_of[c][:], func=ACT.Tanh,
                 bias=bias_ih[:, n_col : n_col + 1], scale=1.0,
             )
+            new_of[c] = new
+
+        def difference(c):
             diff = work.tile([P, CHUNK], F32)
-            blend_engine(c).tensor_tensor(out=diff[:], in0=new[:], in1=ht_of[c][:], op=ALU.subtract)
+            blend_engine(c).tensor_tensor(
+                out=diff[:], in0=new_of[c][:], in1=ht_of[c][:], op=ALU.subtract
+            )
             diff_of[c] = diff
 
         def blend(c):
@@ -332,9 +340,13 @@ def tile_grouptorchgru_t_e_kernel(
             run(matmul_hidden, i - BEHIND_CAND, NEW)
             run(copy_hidden_reset, i)
             run(candidate, i - BEHIND_BLEND)
+            if on_gpsimd(i - BEHIND_BLEND):
+                run(difference, i - BEHIND_BLEND)
             run(sum_reset, i)
             run(copy_inputs_update, i)
             run(gate_hidden, i - BEHIND_CAND)
+            if not on_gpsimd(i - BEHIND_BLEND):
+                run(difference, i - BEHIND_BLEND)
             if i == 0:
                 transpose_inputs(1, 0, nc.scalar.copy)
                 transpose_inputs(1, 1, nc.vector.tensor_copy)
@@ -348,6 +360,9 @@ def tile_grouptorchgru_t_e_kernel(
             run(transpose_inputs, i + AHEAD_IN, 1, nc.vector.tensor_copy)
             if i == 0:
                 quantise(1)
+            if not on_gpsimd(i - BEHIND_BLEND):
+                run(blend, i - BEHIND_BLEND)
             run(transpose_out, i - BEHIND_OUT)
             run(quantise, i + AHEAD_IN)
-            run(blend, i - BEHIND_BLEND)
+            if on_gpsimd(i - BEHIND_BLEND):
+                run(blend, i - BEHIND_BLEND)

from contextlib import ExitStack

import concourse.mybir as mybir
from concourse.masks import make_identity

F32 = mybir.dt.float32
BF16 = mybir.dt.bfloat16
I32 = mybir.dt.int32
U32 = mybir.dt.uint32
U8 = mybir.dt.uint8
FP8X4 = mybir.dt.float8_e4m3fn_x4
ACT = mybir.ActivationFunctionType
ALU = mybir.AluOpType

BATCH, UNITS, K_IN, HID = 4096, 4, 512, 128
P = 128
GATES = 3
RESET, UPDATE, NEW = 0, 1, 2
ROW_GROUPS = 4
CHUNK = P * ROW_GROUPS
N_CHUNKS = (BATCH // CHUNK) * UNITS
WORDS = K_IN // 2
HALF = CHUNK // 2

AHEAD_LOAD = 4
AHEAD_IN = 2
BEHIND_CAND = 1
BEHIND_BLEND = 2
BEHIND_OUT = 3

FLOPS = 2 * BATCH * UNITS * (K_IN + HID) * GATES * HID


def tile_grouptorchgru_t_e_kernel(
    tc, inputs, hidden, w_ih_words, w_ih_scales, w_hh, b_ih, b_hh, out
):
    nc = tc.nc
    with ExitStack() as ctx:
        ctx.enter_context(tc.manual_schedule())
        const = ctx.enter_context(tc.tile_pool(name="const", bufs=1))
        x_pool = ctx.enter_context(tc.tile_pool(name="x", bufs=4))
        hid_pool = ctx.enter_context(tc.tile_pool(name="hid", bufs=4))
        mx_pool = ctx.enter_context(tc.tile_pool(name="mx", bufs=5))
        ht_pool = ctx.enter_context(tc.tile_pool(name="ht", bufs=6))
        work = ctx.enter_context(tc.tile_pool(name="work", bufs=2))
        late = ctx.enter_context(tc.tile_pool(name="late", bufs=4))
        mid = ctx.enter_context(tc.tile_pool(name="mid", bufs=3))
        psum = ctx.enter_context(tc.psum_pool(name="psum", bufs=8))

        x_of, hid_of, grouped_of, codes_of, planes_of, ht_of = {}, {}, {}, {}, {}, {}
        gh_of, gx_of, pre_of, gated_of, cand_of, blend_of = {}, {}, {}, {}, {}, {}
        xz_ps_of, xz_of, z_ps_of, reset_of, keep_of, new_of, diff_of = {}, {}, {}, {}, {}, {}, {}

        def batch_rows(c):
            first = (c // UNITS) * CHUNK
            return slice(first, first + CHUNK)

        def load(c):
            block, u = divmod(c, UNITS)
            x = x_pool.tile([P, ROW_GROUPS, K_IN], BF16)
            nc.sync.dma_start(
                out=x[:],
                in_=inputs[batch_rows(c), u, :].rearrange("(p j) k -> p j k", j=ROW_GROUPS),
            )
            x_of[c] = x
            if u == 0:
                hid = hid_pool.tile([P, ROW_GROUPS, UNITS, HID], BF16)
                nc.sync.dma_start(
                    out=hid[:],
                    in_=hidden[batch_rows(c), :, :].rearrange("(p j) u h -> p j u h", j=ROW_GROUPS),
                )
                hid_of[block] = hid

        def transpose_inputs(c, half, copy):
            if half == 0:
                grouped = work.tile([P, CHUNK * 4], BF16, align_bytes=64)
                grouped_of[c] = grouped
            x_words = x_of[c][:].bitcast(F32)
            grouped_words = grouped_of[c][:].bitcast(F32).rearrange("p (r w) -> p r w", w=2)
            xt = psum.tile([P, 2, HALF], F32, tag="bank")
            for jj in range(2):
                for w in range(2):
                    nc.tensor.transpose(
                        xt[:, w, jj * P : (jj + 1) * P],
                        x_words[:, 2 * half + jj, w:WORDS:2],
                        ident_f32[:],
                    )
            copy(
                out=grouped_words[:, half * HALF : (half + 1) * HALF, :],
                in_=xt[:].rearrange("p w r -> p r w"),
            )

        def transpose_hidden(c, copy):
            block, u = divmod(c, UNITS)
            ht_ps = psum.tile([P, CHUNK], BF16, tag="bank")
            for j in range(ROW_GROUPS):
                nc.tensor.transpose(
                    ht_ps[:, j * P : (j + 1) * P], hid_of[block][:, j, u, :], ident_bf[:]
                )
            ht = ht_pool.tile([P, CHUNK], BF16)
            copy(out=ht[:], in_=ht_ps[:])
            ht_of[c] = ht

        def quantise(c):
            codes = mx_pool.tile([P, CHUNK], U32, align_bytes=64)
            planes = mx_pool.tile([P, CHUNK], U8, align_bytes=64)
            nc.vector.quantize_mx(
                out=codes[:].bitcast(FP8X4), scales=planes[:], in_=grouped_of[c][:]
            )
            codes_of[c] = codes
            planes_of[c] = planes

        def matmul_hidden(c, gate):
            u = c % UNITS
            gh = psum.tile([P, CHUNK], F32, tag="bank")
            nc.tensor.matmul(
                out=gh[:], lhsT=whh_t[:, u * GATES + gate, :], rhs=ht_of[c][:], start=True, stop=True
            )
            gh_of[c, gate] = gh

        def matmul_inputs(c, gate):
            u = c % UNITS
            cols = slice(gate * HID, (gate + 1) * HID)
            gx = psum.tile([P, CHUNK], F32, tag="bank")
            nc.tensor.matmul_mx(
                out=gx[:],
                lhsT=w_words[:, u, cols].bitcast(FP8X4),
                lhsT_scale=w_planes[:, u, cols],
                rhs=codes_of[c][:].bitcast(FP8X4),
                rhs_scale=planes_of[c][:],
                start=True,
                stop=True,
            )
            gx_of[c, gate] = gx

        def matmul_inputs_update(c):
            u = c % UNITS
            cols = slice(UPDATE * HID, (UPDATE + 1) * HID)
            xz_ps = psum.tile([P, ROW_GROUPS, HID], F32, tag="bank")
            for j in range(ROW_GROUPS):
                rows = slice(j * P, (j + 1) * P)
                nc.tensor.matmul_mx(
                    out=xz_ps[:, j, :],
                    lhsT=codes_of[c][:, rows].bitcast(FP8X4),
                    lhsT_scale=planes_of[c][:, rows],
                    rhs=w_words[:, u, cols].bitcast(FP8X4),
                    rhs_scale=w_planes[:, u, cols],
                    start=True,
                    stop=True,
                )
            xz_ps_of[c] = xz_ps

        def copy_inputs_update(c):
            xz = mid.tile([P, ROW_GROUPS, HID], F32)
            nc.scalar.copy(out=xz[:], in_=xz_ps_of[c][:])
            xz_of[c] = xz

        def sum_update(c):
            u = c % UNITS
            z_ps = psum.tile([P, CHUNK], F32, tag="bank")
            nc.tensor.matmul(
                out=z_ps[:], lhsT=whh_t[:, u * GATES + UPDATE, :], rhs=ht_of[c][:],
                start=True, stop=False,
            )
            for j in range(ROW_GROUPS):
                nc.tensor.matmul(
                    out=z_ps[:, j * P : (j + 1) * P], lhsT=xz_of[c][:, j, :], rhs=ident_f32[:],
                    is_transpose=True, start=False, stop=(j == ROW_GROUPS - 1),
                )
            z_ps_of[c] = z_ps

        def sigmoid_update(c):
            z_col = (c % UNITS) * GATES + UPDATE
            keep = late.tile([P, CHUNK], F32)
            nc.scalar.activation(
                out=keep[:], in_=z_ps_of[c][:], func=ACT.Sigmoid,
                bias=bias_neg[:, z_col : z_col + 1], scale=-1.0,
            )
            keep_of[c] = keep

        def copy_hidden_reset(c):
            r_col = (c % UNITS) * GATES + RESET
            pre = work.tile([P, CHUNK], F32)
            nc.scalar.activation(
                out=pre[:], in_=gh_of[c, RESET][:], func=ACT.Identity,
                bias=bias_sum[:, r_col : r_col + 1], scale=1.0,
            )
            pre_of[c] = pre

        def sum_reset(c):
            nc.vector.tensor_tensor(
                out=pre_of[c][:], in0=pre_of[c][:], in1=gx_of[c, RESET][:], op=ALU.add
            )

        def sigmoid_reset(c):
            reset = mid.tile([P, CHUNK], F32)
            nc.scalar.activation(out=reset[:], in_=pre_of[c][:], func=ACT.Sigmoid)
            reset_of[c] = reset

        def gate_hidden(c):
            n_col = (c % UNITS) * GATES + NEW
            gated = work.tile([P, CHUNK], F32)
            nc.vector.scalar_tensor_tensor(
                out=gated[:], in0=gh_of[c, NEW][:], scalar=bias_hh[:, n_col : n_col + 1],
                in1=reset_of[c][:], op0=ALU.add, op1=ALU.mult,
            )
            gated_of[c] = gated

        def sum_candidate(c):
            cand = work.tile([P, CHUNK], F32)
            nc.vector.tensor_tensor(
                out=cand[:], in0=gated_of[c][:], in1=gx_of[c, NEW][:], op=ALU.add
            )
            cand_of[c] = cand

        def on_gpsimd(c):
            return c < N_CHUNKS - 2

        def blend_engine(c):
            return nc.gpsimd if on_gpsimd(c) else nc.vector

        def candidate(c):
            n_col = (c % UNITS) * GATES + NEW
            new = work.tile([P, CHUNK], F32)
            nc.scalar.activation(
                out=new[:], in_=cand_of[c][:], func=ACT.Tanh,
                bias=bias_ih[:, n_col : n_col + 1], scale=1.0,
            )
            new_of[c] = new

        def difference(c):
            diff = work.tile([P, CHUNK], F32)
            blend_engine(c).tensor_tensor(
                out=diff[:], in0=new_of[c][:], in1=ht_of[c][:], op=ALU.subtract
            )
            diff_of[c] = diff

        def blend(c):
            mixed = late.tile([P, CHUNK], F32)
            blend_engine(c).tensor_tensor(out=mixed[:], in0=keep_of[c][:], in1=diff_of[c][:], op=ALU.mult)
            blend_of[c] = mixed

        def transpose_out(c):
            block, u = divmod(c, UNITS)
            back = psum.tile([P, ROW_GROUPS, HID], F32, tag="bank")
            for j in range(ROW_GROUPS):
                nc.tensor.transpose(
                    back[:, j, :], blend_of[c][:, j * P : (j + 1) * P], ident_f32[:]
                )
            result = late.tile([P, ROW_GROUPS, HID], F32)
            nc.vector.tensor_tensor(
                out=result[:], in0=back[:], in1=hid_of[block][:, :, u, :], op=ALU.add
            )
            nc.sync.dma_start(
                out=out[batch_rows(c), u, :].rearrange("(p j) h -> p j h", j=ROW_GROUPS),
                in_=result[:],
            )

        def run(stage, c, *args):
            if 0 <= c < N_CHUNKS:
                stage(c, *args)

        warm = const.tile([P, 1], F32)
        nc.vector.memset(warm[:], 0.0)
        nc.scalar.activation(out=warm[:], in_=warm[:], func=ACT.Sigmoid)

        ident_f32 = const.tile([P, P], F32)
        make_identity(nc, ident_f32[:])
        ident_bf = const.tile([P, P], BF16)
        make_identity(nc, ident_bf[:])

        w_planes = const.tile([P, UNITS, GATES * HID], U8, align_bytes=64)
        nc.vector.memset(w_planes[:].bitcast(I32), 0)
        bias_rows = const.tile([P, P], BF16)
        nc.vector.memset(bias_rows[:], 0.0)

        load(0)
        whh_rows = const.tile([P, UNITS * GATES, HID], BF16)
        nc.sync.dma_start(out=whh_rows[:], in_=w_hh.rearrange("u (g m) k -> m (u g) k", m=P))
        n_bias = UNITS * GATES
        nc.sync.dma_start(out=bias_rows[0:n_bias, :], in_=b_ih.rearrange("u (g h) -> (u g) h", h=HID))
        nc.sync.dma_start(
            out=bias_rows[n_bias : 2 * n_bias, :], in_=b_hh.rearrange("u (g h) -> (u g) h", h=HID)
        )
        for quadrant in range(4):
            nc.sync.dma_start(
                out=w_planes[32 * quadrant : 32 * quadrant + 4, :, :].bitcast(I32),
                in_=w_ih_scales[:, 4 * quadrant : 4 * quadrant + 4, :]
                .rearrange("u q n -> q u n")
                .bitcast(I32),
            )
        w_words = const.tile([P, UNITS, GATES * HID], U32, align_bytes=64)

        def load_words(u):
            nc.sync.dma_start(
                out=w_words[:, u, :].bitcast(I32),
                in_=w_ih_words[u].rearrange("p n t -> p (n t)").bitcast(I32),
            )

        load_words(0)
        load(1)
        load(2)
        for u in range(1, UNITS):
            load_words(u)
        load(3)

        transpose_inputs(0, 0, nc.scalar.copy)
        transpose_hidden(0, nc.scalar.copy)
        transpose_inputs(0, 1, nc.vector.tensor_copy)
        quantise(0)

        whh_t = const.tile([P, UNITS * GATES, P], BF16)
        bias_ih = const.tile([P, n_bias], F32)
        bias_hh = const.tile([P, n_bias], F32)
        bias_sum = const.tile([P, n_bias], F32)
        bias_neg = const.tile([P, n_bias], F32)

        def prepare_weights():
            for u in range(UNITS):
                whh_ps = psum.tile([P, GATES, P], BF16, tag="bank")
                for gate in range(GATES):
                    nc.tensor.transpose(
                        whh_ps[:, gate, :], whh_rows[:, u * GATES + gate, :], ident_bf[:]
                    )
                nc.vector.tensor_copy(out=whh_t[:, u * GATES : (u + 1) * GATES, :], in_=whh_ps[:])
            bias_ps = psum.tile([P, P], BF16, tag="bank")
            nc.tensor.transpose(bias_ps[:], bias_rows[:], ident_bf[:])
            nc.vector.tensor_copy(out=bias_ih[:], in_=bias_ps[:, 0:n_bias])
            nc.vector.tensor_copy(out=bias_hh[:], in_=bias_ps[:, n_bias : 2 * n_bias])
            nc.vector.tensor_tensor(out=bias_sum[:], in0=bias_ih[:], in1=bias_hh[:], op=ALU.add)
            nc.vector.tensor_scalar_mul(out=bias_neg[:], in0=bias_sum[:], scalar1=-1.0)

        prepare_weights()
        for i in range(N_CHUNKS + BEHIND_OUT):
            run(load, i + AHEAD_LOAD)
            run(matmul_hidden, i, RESET)
            run(matmul_inputs, i, RESET)
            run(matmul_inputs_update, i)
            run(matmul_inputs, i - BEHIND_CAND, NEW)
            run(matmul_hidden, i - BEHIND_CAND, NEW)
            run(copy_hidden_reset, i)
            run(candidate, i - BEHIND_BLEND)
            if on_gpsimd(i - BEHIND_BLEND):
                run(difference, i - BEHIND_BLEND)
            run(sum_reset, i)
            run(copy_inputs_update, i)
            run(gate_hidden, i - BEHIND_CAND)
            if not on_gpsimd(i - BEHIND_BLEND):
                run(difference, i - BEHIND_BLEND)
            if i == 0:
                transpose_inputs(1, 0, nc.scalar.copy)
                transpose_inputs(1, 1, nc.vector.tensor_copy)
                transpose_hidden(1, nc.scalar.copy)
            run(transpose_inputs, i + AHEAD_IN, 0, nc.scalar.copy)
            run(transpose_hidden, i + AHEAD_IN, nc.vector.tensor_copy)
            run(sum_candidate, i - BEHIND_CAND)
            run(sigmoid_reset, i)
            run(sum_update, i - BEHIND_CAND)
            run(sigmoid_update, i - BEHIND_CAND)
            run(transpose_inputs, i + AHEAD_IN, 1, nc.vector.tensor_copy)
            if i == 0:
                quantise(1)
            if not on_gpsimd(i - BEHIND_BLEND):
                run(blend, i - BEHIND_BLEND)
            run(transpose_out, i - BEHIND_OUT)
            run(quantise, i + AHEAD_IN)
            if on_gpsimd(i - BEHIND_BLEND):
                run(blend, i - BEHIND_BLEND)
